import numpy as np
import ml_dtypes


def mxq(x, axis, fmt="e4m3"):
    dtype, down = {"e4m3": (ml_dtypes.float8_e4m3fn, 7), "e5m2": (ml_dtypes.float8_e5m2, 14)}[fmt]
    v = np.moveaxis(np.asarray(x, np.float32).astype(ml_dtypes.bfloat16).astype(np.float64), axis, -1)
    blocks = v.reshape(v.shape[:-1] + (-1, 32))
    amax = np.abs(blocks).max(-1, keepdims=True)
    byte = np.maximum(np.where(amax > 0, np.frexp(amax)[1] - 1 + 127, 0) - down, 1)
    scale = np.exp2(byte - 127.0)
    codes = (blocks / scale).astype(np.float32).astype(dtype).astype(np.float64)
    return np.moveaxis((codes * scale).reshape(v.shape), -1, axis)


WIDE = False


def mx_kscale(k):
    if not WIDE:
        return np.ones(k)
    levels = np.array([20, -20, 10, -10, 0])
    a = np.random.permutation(np.resize(levels, k // 512 * 4)).reshape(k // 512, 4)
    idx = np.arange(k)
    return np.exp2(a[idx // 512, idx % 128 // 32])


BF16 = ml_dtypes.bfloat16


def bf(x):
    return np.asarray(x, np.float32).astype(BF16)


def f64(x):
    return np.asarray(x).astype(np.float64)


B, D, U, R = 3072, 512, 512, 8
EPS = 1e-12


def softplus(v):
    return np.maximum(v, 0.0) + np.log(1.0 + np.exp(-np.abs(v)))


def draw(n, p):
    v = 0.3 * np.random.standard_normal((n, D)) / np.sqrt(D)
    for r in range(R):
        v = v + 0.8 * np.random.standard_normal((n, 1)) * p[r] / np.sqrt(R * D)
    return v


def setup_inputs():
    s = mx_kscale(B)
    p = np.random.standard_normal((R, D))
    x0 = bf(draw(B, p))
    c0 = bf(draw(U, p))
    gamma_raw = bf(np.log(np.exp(1.0) - 1.0) + 0.3 * np.random.standard_normal(U))
    g = bf(8.0 * np.random.standard_normal((B, U)) * np.exp2(np.random.randint(-12, 1, (B, 1))) / s[:, None])
    xf, cf = f64(x0), f64(c0)
    x_norm = np.sum(np.square(xf), axis=-1, keepdims=True)
    c_norm = np.sum(np.square(cf), axis=-1)
    d2 = np.maximum(x_norm - 2.0 * (xf @ cf.T) + c_norm[None, :] + EPS, 0.0)
    return {"x": bf(xf * s[:, None]), "centers": bf(cf * s.min()), "gamma_raw": gamma_raw,
            "d2": np.asarray(d2, np.float32), "grad_out": g}


def reference(x, centers, gamma_raw, d2, grad_out):
    x, centers, d2 = f64(x), f64(centers), f64(d2)
    gamma = softplus(f64(gamma_raw))[None, :]
    dz = np.where(d2 > 0.0, -f64(grad_out) * gamma * np.exp(-gamma * d2), 0.0)
    m = mxq(dz, 0, "e5m2").T @ mxq(x, 0, "e4m3")
    return -2.0 * m + 2.0 * centers * np.sum(dz, axis=0)[:, None]

@@ -1,0 +1,276 @@
+from contextlib import ExitStack
+
+import concourse.mybir as mybir
+from concourse.masks import make_identity
+
+F32 = mybir.dt.float32
+BF16 = mybir.dt.bfloat16
+U32 = mybir.dt.uint32
+U8 = mybir.dt.uint8
+E4M3_X4 = mybir.dt.float8_e4m3fn_x4
+E5M2_X4 = mybir.dt.float8_e5m2_x4
+ALU = mybir.AluOpType
+ACT = mybir.ActivationFunctionType
+
+ROWS = 3072
+UNITS = 512
+FEATURES = 512
+P = 128
+PACK = 4
+K_PASS = P * PACK
+ROUNDS = ROWS // K_PASS
+UNIT_BLOCKS = UNITS // P
+PAIR = 2
+STEP_COLS = PAIR * P
+STEPS_PER_ROUND = UNIT_BLOCKS // PAIR
+STEPS = ROUNDS * STEPS_PER_ROUND
+X_VECTOR_COLS = 64
+
+FLOPS = 2 * ROWS * UNITS * FEATURES
+
+
+def tile_rbflayer_v_kernel(tc, x, centers, gamma_raw, d2, grad_out, out):
+    nc = tc.nc
+    with ExitStack() as stack:
+        const = stack.enter_context(tc.tile_pool(name="const", bufs=1))
+        loaded = stack.enter_context(tc.tile_pool(name="loaded", bufs=ROUNDS))
+        work = stack.enter_context(tc.tile_pool(name="work", bufs=2))
+        psum_out = stack.enter_context(tc.psum_pool(name="psum_out", bufs=1))
+        psum_d2 = stack.enter_context(tc.psum_pool(name="psum_d2", bufs=PAIR))
+        psum_grad = stack.enter_context(tc.psum_pool(name="psum_grad", bufs=1))
+        psum_back = stack.enter_context(tc.psum_pool(name="psum_back", bufs=1))
+        stack.enter_context(tc.manual_schedule())
+
+        gamma_rows = const.tile([P, P], BF16)
+        nc.vector.memset(gamma_rows[:], 0.0)
+        nc.sync.dma_start(
+            out=gamma_rows[0:UNIT_BLOCKS, :], in_=gamma_raw.rearrange("(m p) -> m p", p=P)
+        )
+        d2_rows, grad_rows, x_rows = [], [], []
+        for c in range(ROUNDS):
+            k_rows = slice(c * K_PASS, (c + 1) * K_PASS)
+            d2_c = loaded.tile([P, PACK, UNITS], F32)
+            nc.sync.dma_start(out=d2_c[:], in_=d2[k_rows, :].rearrange("(p j) u -> p j u", j=PACK))
+            grad_c = loaded.tile([P, PACK, UNITS], BF16)
+            nc.sync.dma_start(
+                out=grad_c[:], in_=grad_out[k_rows, :].rearrange("(p j) u -> p j u", j=PACK)
+            )
+            x_c = loaded.tile([P, PACK, FEATURES], BF16)
+            nc.sync.dma_start(out=x_c[:], in_=x[k_rows, :].rearrange("(p j) i -> p j i", j=PACK))
+            d2_rows.append(d2_c)
+            grad_rows.append(grad_c)
+            x_rows.append(x_c)
+        centers_sb = const.tile([P, UNIT_BLOCKS, FEATURES], BF16)
+        nc.sync.dma_start(out=centers_sb[:], in_=centers.rearrange("(m p) i -> p m i", p=P))
+
+        ident_bf16 = const.tile([P, P], BF16)
+        make_identity(nc, ident_bf16[:])
+        ident_f32 = const.tile([P, P], F32)
+        make_identity(nc, ident_f32[:])
+
+        gamma_cols = psum_back.tile([P, P], BF16, tag="back")
+        nc.tensor.transpose(gamma_cols[:], gamma_rows[:], ident_bf16[:])
+        raw = const.tile([P, UNIT_BLOCKS], F32)
+        nc.vector.tensor_copy(out=raw[:], in_=gamma_cols[:, 0:UNIT_BLOCKS])
+        magnitude = const.tile([P, UNIT_BLOCKS], F32)
+        nc.scalar.activation(out=magnitude[:], in_=raw[:], func=ACT.Abs)
+        decay = const.tile([P, UNIT_BLOCKS], F32)
+        nc.scalar.activation(out=decay[:], in_=magnitude[:], func=ACT.Exp, scale=-1.0)
+        log_term = const.tile([P, UNIT_BLOCKS], F32)
+        nc.scalar.activation(out=log_term[:], in_=decay[:], func=ACT.Ln, bias=1.0)
+        gamma = const.tile([P, UNIT_BLOCKS], F32)
+        nc.vector.scalar_tensor_tensor(
+            out=gamma[:], in0=raw[:], scalar=0.0, in1=log_term[:], op0=ALU.max, op1=ALU.add
+        )
+        neg_gamma = const.tile([P, UNIT_BLOCKS], F32)
+        nc.vector.tensor_scalar_mul(out=neg_gamma[:], in0=gamma[:], scalar1=-1.0)
+
+        dz_codes = const.tile([P, ROUNDS, UNITS], U32, align_bytes=64)
+        dz_scales = const.tile([P, ROUNDS, UNITS], U8, align_bytes=64)
+        x_codes = const.tile([P, ROUNDS, FEATURES], U32, align_bytes=64)
+        x_scales = const.tile([P, ROUNDS, FEATURES], U8, align_bytes=64)
+        row_sums = const.tile([P, UNIT_BLOCKS, ROUNDS], F32)
+        products = []
+        for m in range(UNIT_BLOCKS):
+            products.append(psum_out.tile([P, FEATURES], F32, name="products%d" % m))
+
+        masked_grad, x_grouped, d2_t, grad_t, decays, dz_t, dz_back, dz_grouped = (
+            {}, {}, {}, {}, {}, {}, {}, {},
+        )
+        center_terms = {}
+
+        def place(s):
+            c, h = divmod(s, STEPS_PER_ROUND)
+            return c, h, slice(h * STEP_COLS, (h + 1) * STEP_COLS)
+
+        def mask_grad(s):
+            c, h, cols = place(s)
+            masked_grad[s] = work.tile([P, PACK, STEP_COLS], BF16, name="masked_grad")
+            nc.vector.scalar_tensor_tensor(
+                out=masked_grad[s][:],
+                in0=d2_rows[c][:, :, cols],
+                scalar=0.0,
+                in1=grad_rows[c][:, :, cols],
+                op0=ALU.is_gt,
+                op1=ALU.mult,
+            )
+
+        def regroup_x(s):
+            c, h, cols = place(s)
+            x_grouped[s] = work.tile([P, STEP_COLS, PACK], BF16, name="x_grouped", align_bytes=64)
+            target = x_grouped[s][:].rearrange("p (n i) j -> p n j i", i=4)
+            source = x_rows[c][:, :, cols].rearrange("p j (n i) -> p n j i", i=4)
+            split = X_VECTOR_COLS // 4
+            nc.vector.tensor_copy(out=target[:, :split], in_=source[:, :split])
+            nc.scalar.copy(out=target[:, split:], in_=source[:, split:])
+
+        def quantise_x(s):
+            c, h, cols = place(s)
+            nc.vector.quantize_mx(
+                out=x_codes[:, c, cols].bitcast(E4M3_X4),
+                scales=x_scales[:, c, cols],
+                in_=x_grouped[s][:].rearrange("p i j -> p (i j)"),
+            )
+
+        def transpose_d2(s):
+            c, h, cols = place(s)
+            for n in range(PAIR):
+                m = h * PAIR + n
+                d2_t[s, n] = psum_d2.tile([P, K_PASS], F32, name="d2_t")
+                for j in range(PACK):
+                    nc.tensor.transpose(
+                        d2_t[s, n][:, j * P : (j + 1) * P],
+                        d2_rows[c][:, j, m * P : (m + 1) * P],
+                        ident_f32[:],
+                    )
+
+        def transpose_grad(s):
+            grad_t[s] = psum_grad.tile([P, PAIR, K_PASS], BF16, name="grad_t")
+            for n in range(PAIR):
+                for j in range(PACK):
+                    nc.tensor.transpose(
+                        grad_t[s][:, n, j * P : (j + 1) * P],
+                        masked_grad[s][:, j, n * P : (n + 1) * P],
+                        ident_bf16[:],
+                    )
+
+        def exponentials(s):
+            c, h, cols = place(s)
+            decays[s] = work.tile([P, PAIR, K_PASS], F32, name="decays")
+            for n in range(PAIR):
+                m = h * PAIR + n
+                nc.scalar.activation(
+                    out=decays[s][:, n, :],
+                    in_=d2_t[s, n][:],
+                    func=ACT.Exp,
+                    scale=neg_gamma[:, m : m + 1],
+                )
+
+        def multiply_dz(s):
+            c, h, cols = place(s)
+            dz_t[s] = work.tile([P, PAIR, K_PASS], BF16, name="dz_t")
+            for n in range(PAIR):
+                m = h * PAIR + n
+                nc.vector.scalar_tensor_tensor(
+                    out=dz_t[s][:, n, :],
+                    in0=decays[s][:, n, :],
+                    scalar=neg_gamma[:, m : m + 1],
+                    in1=grad_t[s][:, n, :],
+                    op0=ALU.mult,
+                    op1=ALU.mult,
+                    accum_out=row_sums[:, m, c : c + 1],
+                )
+
+        def transpose_back(s):
+            dz_back[s] = psum_back.tile([P, PACK, STEP_COLS], BF16, name="dz_back", tag="back")
+            for n in range(PAIR):
+                for j in range(PACK):
+                    nc.tensor.transpose(
+                        dz_back[s][:, j, n * P : (n + 1) * P],
+                        dz_t[s][:, n, j * P : (j + 1) * P],
+                        ident_bf16[:],
+                    )
+
+        def regroup_dz(s):
+            dz_grouped[s] = work.tile([P, STEP_COLS, PACK], BF16, name="dz_grouped", align_bytes=64)
+            nc.scalar.copy(out=dz_grouped[s][:], in_=dz_back[s][:].rearrange("p j u -> p u j"))
+
+        def quantise_dz(s):
+            c, h, cols = place(s)
+            nc.vector.quantize_mx(
+                out=dz_codes[:, c, cols].bitcast(E5M2_X4),
+                scales=dz_scales[:, c, cols],
+                in_=dz_grouped[s][:].rearrange("p u j -> p (u j)"),
+            )
+
+        def matmul_round(s):
+            c, h, cols = place(s)
+            for n in range(PAIR):
+                m = h * PAIR + n
+                unit_cols = slice(m * P, (m + 1) * P)
+                nc.tensor.matmul_mx(
+                    out=products[m][:],
+                    lhsT=dz_codes[:, c, unit_cols].bitcast(E5M2_X4),
+                    lhsT_scale=dz_scales[:, c, unit_cols],
+                    rhs=x_codes[:, c, :].bitcast(E4M3_X4),
+                    rhs_scale=x_scales[:, c, :],
+                    start=(c == 0),
+                    stop=(c == ROUNDS - 1),
+                )
+
+        def center_term(s):
+            c, h, cols = place(s)
+            blocks = slice(h * PAIR, (h + 1) * PAIR)
+            totals = work.tile([P, PAIR], F32, name="totals")
+            nc.vector.tensor_reduce(
+                out=totals[:], in_=row_sums[:, blocks, :], axis=mybir.AxisListType.X, op=ALU.add
+            )
+            doubled = work.tile([P, PAIR], F32, name="doubled")
+            nc.vector.tensor_scalar_mul(out=doubled[:], in0=totals[:], scalar1=2.0)
+            for n in range(PAIR):
+                m = h * PAIR + n
+                center_terms[m] = work.tile([P, FEATURES], F32, name="center_term", bufs=UNIT_BLOCKS)
+                nc.scalar.activation(
+                    out=center_terms[m][:],
+                    in_=centers_sb[:, m, :],
+                    func=ACT.Copy,
+                    scale=doubled[:, n : n + 1],
+                )
+
+        def store_out(s):
+            c, h, cols = place(s)
+            for n in range(PAIR):
+                m = h * PAIR + n
+                result = work.tile([P, FEATURES], F32, name="result", bufs=UNIT_BLOCKS)
+                nc.vector.scalar_tensor_tensor(
+                    out=result[:],
+                    in0=products[m][:],
+                    scalar=-2.0,
+                    in1=center_terms[m][:],
+                    op0=ALU.mult,
+                    op1=ALU.add,
+                )
+                nc.sync.dma_start(out=out[m * P : (m + 1) * P, :], in_=result[:])
+
+        def run(stage, s):
+            if 0 <= s < STEPS:
+                stage(s)
+
+        def run_last_round(stage, s):
+            if STEPS - STEPS_PER_ROUND <= s < STEPS:
+                stage(s)
+
+        for t in range(-2, STEPS + 1):
+            run(multiply_dz, t)
+            run(transpose_back, t)
+            run(transpose_grad, t + 1)
+            run(quantise_dz, t - 1)
+            run(matmul_round, t - 1)
+            run_last_round(store_out, t - 1)
+            run(quantise_x, t + 1)
+            run(mask_grad, t + 2)
+            run(regroup_x, t + 2)
+            run(exponentials, t + 1)
+            run(regroup_dz, t)
+            run_last_round(center_term, t)
+            run(transpose_d2, t + 2)

@@ -265,12 +265,12 @@ def tile_rbflayer_v_kernel(tc, x, centers, gamma_raw, d2, grad_out, out):
             run(transpose_back, t)
             run(transpose_grad, t + 1)
             run(quantise_dz, t - 1)
+            run(quantise_x, t)
             run(matmul_round, t - 1)
             run_last_round(store_out, t - 1)
-            run(quantise_x, t + 1)
             run(mask_grad, t + 2)
-            run(regroup_x, t + 2)
             run(exponentials, t + 1)
             run(regroup_dz, t)
+            run(regroup_x, t + 1)
             run_last_round(center_term, t)
             run(transpose_d2, t + 2)

@@ -24,7 +24,7 @@ PAIR = 2
 STEP_COLS = PAIR * P
 STEPS_PER_ROUND = UNIT_BLOCKS // PAIR
 STEPS = ROUNDS * STEPS_PER_ROUND
-X_VECTOR_COLS = 64
+X_VECTOR_COLS = 128
 
 FLOPS = 2 * ROWS * UNITS * FEATURES
 
@@ -98,21 +98,32 @@ def tile_rbflayer_v_kernel(tc, x, centers, gamma_raw, d2, grad_out, out):
             {}, {}, {}, {}, {}, {}, {}, {},
         )
         center_terms = {}
+        positive = {}
 
         def place(s):
             c, h = divmod(s, STEPS_PER_ROUND)
             return c, h, slice(h * STEP_COLS, (h + 1) * STEP_COLS)
 
+        def compare_d2(s):
+            c, h, cols = place(s)
+            positive[s] = work.tile([P, PACK, STEP_COLS], BF16, name="positive", bufs=3)
+            nc.gpsimd.tensor_scalar(
+                out=positive[s][:],
+                in0=d2_rows[c][:, :, cols],
+                scalar1=0.0,
+                scalar2=1.0,
+                op0=ALU.is_gt,
+                op1=ALU.mult,
+            )
+
         def mask_grad(s):
             c, h, cols = place(s)
             masked_grad[s] = work.tile([P, PACK, STEP_COLS], BF16, name="masked_grad")
-            nc.vector.scalar_tensor_tensor(
+            nc.vector.tensor_tensor(
                 out=masked_grad[s][:],
-                in0=d2_rows[c][:, :, cols],
-                scalar=0.0,
+                in0=positive[s][:],
                 in1=grad_rows[c][:, :, cols],
-                op0=ALU.is_gt,
-                op1=ALU.mult,
+                op=ALU.mult,
             )
 
         def regroup_x(s):
@@ -260,7 +271,8 @@ def tile_rbflayer_v_kernel(tc, x, centers, gamma_raw, d2, grad_out, out):
             if STEPS - STEPS_PER_ROUND <= s < STEPS:
                 stage(s)
 
-        for t in range(-2, STEPS + 1):
+        for t in range(-3, STEPS + 1):
+            run(compare_d2, t + 3)
             run(multiply_dz, t)
             run(transpose_back, t)
             run(transpose_grad, t + 1)

@@ -24,7 +24,7 @@ PAIR = 2
 STEP_COLS = PAIR * P
 STEPS_PER_ROUND = UNIT_BLOCKS // PAIR
 STEPS = ROUNDS * STEPS_PER_ROUND
-X_VECTOR_COLS = 128
+X_VECTOR_COLS = 96
 
 FLOPS = 2 * ROWS * UNITS * FEATURES
 
@@ -98,32 +98,21 @@ def tile_rbflayer_v_kernel(tc, x, centers, gamma_raw, d2, grad_out, out):
             {}, {}, {}, {}, {}, {}, {}, {},
         )
         center_terms = {}
-        positive = {}
 
         def place(s):
             c, h = divmod(s, STEPS_PER_ROUND)
             return c, h, slice(h * STEP_COLS, (h + 1) * STEP_COLS)
 
-        def compare_d2(s):
-            c, h, cols = place(s)
-            positive[s] = work.tile([P, PACK, STEP_COLS], BF16, name="positive", bufs=3)
-            nc.gpsimd.tensor_scalar(
-                out=positive[s][:],
-                in0=d2_rows[c][:, :, cols],
-                scalar1=0.0,
-                scalar2=1.0,
-                op0=ALU.is_gt,
-                op1=ALU.mult,
-            )
-
         def mask_grad(s):
             c, h, cols = place(s)
             masked_grad[s] = work.tile([P, PACK, STEP_COLS], BF16, name="masked_grad")
-            nc.vector.tensor_tensor(
+            nc.vector.scalar_tensor_tensor(
                 out=masked_grad[s][:],
-                in0=positive[s][:],
+                in0=d2_rows[c][:, :, cols],
+                scalar=0.0,
                 in1=grad_rows[c][:, :, cols],
-                op=ALU.mult,
+                op0=ALU.is_gt,
+                op1=ALU.mult,
             )
 
         def regroup_x(s):
@@ -271,18 +260,17 @@ def tile_rbflayer_v_kernel(tc, x, centers, gamma_raw, d2, grad_out, out):
             if STEPS - STEPS_PER_ROUND <= s < STEPS:
                 stage(s)
 
-        for t in range(-3, STEPS + 1):
-            run(compare_d2, t + 3)
+        for t in range(-2, STEPS + 1):
             run(multiply_dz, t)
             run(transpose_back, t)
             run(transpose_grad, t + 1)
             run(quantise_dz, t - 1)
             run(quantise_x, t)
-            run(matmul_round, t - 1)
-            run_last_round(store_out, t - 1)
             run(mask_grad, t + 2)
             run(exponentials, t + 1)
             run(regroup_dz, t)
             run(regroup_x, t + 1)
             run_last_round(center_term, t)
             run(transpose_d2, t + 2)
+            run(matmul_round, t - 1)
+            run_last_round(store_out, t - 1)

@@ -24,7 +24,11 @@ PAIR = 2
 STEP_COLS = PAIR * P
 STEPS_PER_ROUND = UNIT_BLOCKS // PAIR
 STEPS = ROUNDS * STEPS_PER_ROUND
-X_VECTOR_COLS = 96
+X_HALVES = STEPS
+ORDER = [(c, h) for c in range(ROUNDS - 2) for h in range(STEPS_PER_ROUND)] + [
+    (c, h) for h in range(STEPS_PER_ROUND) for c in range(ROUNDS - 2, ROUNDS)
+]
+X_VECTOR_COLS = 48
 
 FLOPS = 2 * ROWS * UNITS * FEATURES
 
@@ -50,13 +54,20 @@ def tile_rbflayer_v_kernel(tc, x, centers, gamma_raw, d2, grad_out, out):
         for c in range(ROUNDS):
             k_rows = slice(c * K_PASS, (c + 1) * K_PASS)
             d2_c = loaded.tile([P, PACK, UNITS], F32)
-            nc.sync.dma_start(out=d2_c[:], in_=d2[k_rows, :].rearrange("(p j) u -> p j u", j=PACK))
             grad_c = loaded.tile([P, PACK, UNITS], BF16)
-            nc.sync.dma_start(
-                out=grad_c[:], in_=grad_out[k_rows, :].rearrange("(p j) u -> p j u", j=PACK)
-            )
             x_c = loaded.tile([P, PACK, FEATURES], BF16)
-            nc.sync.dma_start(out=x_c[:], in_=x[k_rows, :].rearrange("(p j) i -> p j i", j=PACK))
+            d2_hbm = d2[k_rows, :].rearrange("(p j) u -> p j u", j=PACK)
+            grad_hbm = grad_out[k_rows, :].rearrange("(p j) u -> p j u", j=PACK)
+            x_hbm = x[k_rows, :].rearrange("(p j) i -> p j i", j=PACK)
+            if c == 0:
+                nc.sync.dma_start(out=d2_c[:, :, :STEP_COLS], in_=d2_hbm[:, :, :STEP_COLS])
+                nc.sync.dma_start(out=x_c[:], in_=x_hbm)
+                nc.sync.dma_start(out=grad_c[:], in_=grad_hbm)
+                nc.sync.dma_start(out=d2_c[:, :, STEP_COLS:], in_=d2_hbm[:, :, STEP_COLS:])
+            else:
+                nc.sync.dma_start(out=d2_c[:], in_=d2_hbm)
+                nc.sync.dma_start(out=grad_c[:], in_=grad_hbm)
+                nc.sync.dma_start(out=x_c[:], in_=x_hbm)
             d2_rows.append(d2_c)
             grad_rows.append(grad_c)
             x_rows.append(x_c)
@@ -78,13 +89,8 @@ def tile_rbflayer_v_kernel(tc, x, centers, gamma_raw, d2, grad_out, out):
         nc.scalar.activation(out=decay[:], in_=magnitude[:], func=ACT.Exp, scale=-1.0)
         log_term = const.tile([P, UNIT_BLOCKS], F32)
         nc.scalar.activation(out=log_term[:], in_=decay[:], func=ACT.Ln, bias=1.0)
-        gamma = const.tile([P, UNIT_BLOCKS], F32)
-        nc.vector.scalar_tensor_tensor(
-            out=gamma[:], in0=raw[:], scalar=0.0, in1=log_term[:], op0=ALU.max, op1=ALU.add
-        )
-        neg_gamma = const.tile([P, UNIT_BLOCKS], F32)
-        nc.vector.tensor_scalar_mul(out=neg_gamma[:], in0=gamma[:], scalar1=-1.0)
-
+        warm = const.tile([P, UNIT_BLOCKS], F32)
+        nc.scalar.activation(out=warm[:], in_=decay[:], func=ACT.Exp)
         dz_codes = const.tile([P, ROUNDS, UNITS], U32, align_bytes=64)
         dz_scales = const.tile([P, ROUNDS, UNITS], U8, align_bytes=64)
         x_codes = const.tile([P, ROUNDS, FEATURES], U32, align_bytes=64)
@@ -97,11 +103,28 @@ def tile_rbflayer_v_kernel(tc, x, centers, gamma_raw, d2, grad_out, out):
         masked_grad, x_grouped, d2_t, grad_t, decays, dz_t, dz_back, dz_grouped = (
             {}, {}, {}, {}, {}, {}, {}, {},
         )
-        center_terms = {}
+        neg_totals = {}
 
         def place(s):
-            c, h = divmod(s, STEPS_PER_ROUND)
+            c, h = ORDER[s]
             return c, h, slice(h * STEP_COLS, (h + 1) * STEP_COLS)
+
+        def parts(s):
+            return [[n] for n in range(PAIR)] if s == STEPS - 1 else [list(range(PAIR))]
+
+        def x_turn(k):
+            if k < STEPS_PER_ROUND:
+                return -STEPS
+            return k - 1 if k < X_HALVES - 4 else k - 2
+
+        def x_place(k):
+            c, h = divmod(k, STEPS_PER_ROUND)
+            return c, slice(h * STEP_COLS, (h + 1) * STEP_COLS)
+
+        def t_cols(j):
+            h, e = divmod(j, 2)
+            block = 2 * e + h
+            return slice(block * P, (block + 1) * P)
 
         def mask_grad(s):
             c, h, cols = place(s)
@@ -115,17 +138,20 @@ def tile_rbflayer_v_kernel(tc, x, centers, gamma_raw, d2, grad_out, out):
                 op1=ALU.mult,
             )
 
-        def regroup_x(s):
-            c, h, cols = place(s)
-            x_grouped[s] = work.tile([P, STEP_COLS, PACK], BF16, name="x_grouped", align_bytes=64)
+        def regroup_x(s, vector_cols):
+            c, cols = x_place(s)
+            x_grouped[s] = work.tile(
+                [P, STEP_COLS, PACK], BF16, name="x_grouped", align_bytes=64, bufs=3
+            )
             target = x_grouped[s][:].rearrange("p (n i) j -> p n j i", i=4)
             source = x_rows[c][:, :, cols].rearrange("p j (n i) -> p n j i", i=4)
-            split = X_VECTOR_COLS // 4
+            split = vector_cols // 4
             nc.vector.tensor_copy(out=target[:, :split], in_=source[:, :split])
-            nc.scalar.copy(out=target[:, split:], in_=source[:, split:])
+            if vector_cols < STEP_COLS:
+                nc.scalar.copy(out=target[:, split:], in_=source[:, split:])
 
         def quantise_x(s):
-            c, h, cols = place(s)
+            c, cols = x_place(s)
             nc.vector.quantize_mx(
                 out=x_codes[:, c, cols].bitcast(E4M3_X4),
                 scales=x_scales[:, c, cols],
@@ -139,7 +165,7 @@ def tile_rbflayer_v_kernel(tc, x, centers, gamma_raw, d2, grad_out, out):
                 d2_t[s, n] = psum_d2.tile([P, K_PASS], F32, name="d2_t")
                 for j in range(PACK):
                     nc.tensor.transpose(
-                        d2_t[s, n][:, j * P : (j + 1) * P],
+                        d2_t[s, n][:, t_cols(j)],
                         d2_rows[c][:, j, m * P : (m + 1) * P],
                         ident_f32[:],
                     )
@@ -149,7 +175,7 @@ def tile_rbflayer_v_kernel(tc, x, centers, gamma_raw, d2, grad_out, out):
             for n in range(PAIR):
                 for j in range(PACK):
                     nc.tensor.transpose(
-                        grad_t[s][:, n, j * P : (j + 1) * P],
+                        grad_t[s][:, n, t_cols(j)],
                         masked_grad[s][:, j, n * P : (n + 1) * P],
                         ident_bf16[:],
                     )
@@ -172,36 +198,53 @@ def tile_rbflayer_v_kernel(tc, x, centers, gamma_raw, d2, grad_out, out):
             for n in range(PAIR):
                 m = h * PAIR + n
                 nc.vector.scalar_tensor_tensor(
-                    out=dz_t[s][:, n, :],
-                    in0=decays[s][:, n, :],
-                    scalar=neg_gamma[:, m : m + 1],
-                    in1=grad_t[s][:, n, :],
+                    out=dz_t[s][:, n, :].rearrange("p (q e) -> p q e", e=2),
+                    in0=decays[s][:, n, :].rearrange("p (e q) -> p q e", e=2),
+                    scalar=two_gamma[:, m : m + 1],
+                    in1=grad_t[s][:, n, :].rearrange("p (e q) -> p q e", e=2),
                     op0=ALU.mult,
                     op1=ALU.mult,
                     accum_out=row_sums[:, m, c : c + 1],
                 )
 
         def transpose_back(s):
-            dz_back[s] = psum_back.tile([P, PACK, STEP_COLS], BF16, name="dz_back", tag="back")
-            for n in range(PAIR):
-                for j in range(PACK):
-                    nc.tensor.transpose(
-                        dz_back[s][:, j, n * P : (n + 1) * P],
-                        dz_t[s][:, n, j * P : (j + 1) * P],
-                        ident_bf16[:],
-                    )
+            dz_back[s] = []
+            for units in parts(s):
+                if s < STEPS - 1:
+                    bank = psum_back.tile([P, K_PASS], F32, name="dz_back", tag="back")
+                else:
+                    bank = psum_d2.tile([P, K_PASS], F32, name="d2_t")
+                width = len(units) * P
+                back = bank[:, : 2 * width].rearrange("p (h u) -> p h u", u=width)
+                for i, n in enumerate(units):
+                    words = dz_t[s][:, n, :].bitcast(F32)
+                    for h in range(PACK // 2):
+                        nc.tensor.transpose(
+                            back[:, h, i * P : (i + 1) * P],
+                            words[:, h * P : (h + 1) * P],
+                            ident_f32[:],
+                        )
+                dz_back[s].append(back)
 
         def regroup_dz(s):
             dz_grouped[s] = work.tile([P, STEP_COLS, PACK], BF16, name="dz_grouped", align_bytes=64)
-            nc.scalar.copy(out=dz_grouped[s][:], in_=dz_back[s][:].rearrange("p j u -> p u j"))
+            for units, back in zip(parts(s), dz_back[s]):
+                target = dz_grouped[s][:, units[0] * P : (units[-1] + 1) * P, :]
+                nc.scalar.copy(
+                    out=target.rearrange("p u j -> p (u j)").bitcast(F32),
+                    in_=back.rearrange("p h u -> p u h"),
+                )
 
         def quantise_dz(s):
             c, h, cols = place(s)
-            nc.vector.quantize_mx(
-                out=dz_codes[:, c, cols].bitcast(E5M2_X4),
-                scales=dz_scales[:, c, cols],
-                in_=dz_grouped[s][:].rearrange("p u j -> p (u j)"),
-            )
+            for units in parts(s):
+                source = dz_grouped[s][:, units[0] * P : (units[-1] + 1) * P, :]
+                unit_cols = slice(cols.start + units[0] * P, cols.start + (units[-1] + 1) * P)
+                nc.vector.quantize_mx(
+                    out=dz_codes[:, c, unit_cols].bitcast(E5M2_X4),
+                    scales=dz_scales[:, c, unit_cols],
+                    in_=source.rearrange("p u j -> p (u j)"),
+                )
 
         def matmul_round(s):
             c, h, cols = place(s)
@@ -225,28 +268,18 @@ def tile_rbflayer_v_kernel(tc, x, centers, gamma_raw, d2, grad_out, out):
             nc.vector.tensor_reduce(
                 out=totals[:], in_=row_sums[:, blocks, :], axis=mybir.AxisListType.X, op=ALU.add
             )
-            doubled = work.tile([P, PAIR], F32, name="doubled")
-            nc.vector.tensor_scalar_mul(out=doubled[:], in0=totals[:], scalar1=2.0)
-            for n in range(PAIR):
-                m = h * PAIR + n
-                center_terms[m] = work.tile([P, FEATURES], F32, name="center_term", bufs=UNIT_BLOCKS)
-                nc.scalar.activation(
-                    out=center_terms[m][:],
-                    in_=centers_sb[:, m, :],
-                    func=ACT.Copy,
-                    scale=doubled[:, n : n + 1],
-                )
+            neg_totals[h] = work.tile([P, PAIR], F32, name="neg_totals")
+            nc.vector.tensor_scalar_mul(out=neg_totals[h][:], in0=totals[:], scalar1=-1.0)
 
-        def store_out(s):
-            c, h, cols = place(s)
-            for n in range(PAIR):
-                m = h * PAIR + n
+        def store_out(blocks):
+            for m in blocks:
+                h, n = divmod(m, PAIR)
                 result = work.tile([P, FEATURES], F32, name="result", bufs=UNIT_BLOCKS)
                 nc.vector.scalar_tensor_tensor(
                     out=result[:],
-                    in0=products[m][:],
-                    scalar=-2.0,
-                    in1=center_terms[m][:],
+                    in0=centers_sb[:, m, :],
+                    scalar=neg_totals[h][:, n : n + 1],
+                    in1=products[m][:],
                     op0=ALU.mult,
                     op1=ALU.add,
                 )
@@ -257,20 +290,40 @@ def tile_rbflayer_v_kernel(tc, x, centers, gamma_raw, d2, grad_out, out):
                 stage(s)
 
         def run_last_round(stage, s):
-            if STEPS - STEPS_PER_ROUND <= s < STEPS:
+            if 0 <= s < STEPS and ORDER[s][0] == ROUNDS - 1:
                 stage(s)
 
+        for k in range(STEPS_PER_ROUND):
+            regroup_x(k, STEP_COLS)
+        gamma = const.tile([P, UNIT_BLOCKS], F32)
+        nc.vector.scalar_tensor_tensor(
+            out=gamma[:], in0=raw[:], scalar=0.0, in1=log_term[:], op0=ALU.max, op1=ALU.add
+        )
+        neg_gamma = const.tile([P, UNIT_BLOCKS], F32)
+        nc.vector.tensor_scalar_mul(out=neg_gamma[:], in0=gamma[:], scalar1=-1.0)
+        two_gamma = const.tile([P, UNIT_BLOCKS], F32)
+        nc.vector.tensor_scalar_mul(out=two_gamma[:], in0=gamma[:], scalar1=2.0)
         for t in range(-2, STEPS + 1):
+            if t == -1:
+                for k in range(STEPS_PER_ROUND):
+                    quantise_x(k)
             run(multiply_dz, t)
             run(transpose_back, t)
             run(transpose_grad, t + 1)
             run(quantise_dz, t - 1)
-            run(quantise_x, t)
+            for k in range(X_HALVES):
+                if x_turn(k) == t - 1:
+                    quantise_x(k)
             run(mask_grad, t + 2)
             run(exponentials, t + 1)
             run(regroup_dz, t)
-            run(regroup_x, t + 1)
+            for k in range(X_HALVES):
+                if x_turn(k) == t:
+                    regroup_x(k, X_VECTOR_COLS)
             run_last_round(center_term, t)
             run(transpose_d2, t + 2)
             run(matmul_round, t - 1)
-            run_last_round(store_out, t - 1)
+            if t == STEPS - 1:
+                store_out([0])
+            elif t == STEPS:
+                store_out(range(1, UNIT_BLOCKS))

@@ -56,18 +56,18 @@ def tile_rbflayer_v_kernel(tc, x, centers, gamma_raw, d2, grad_out, out):
             d2_c = loaded.tile([P, PACK, UNITS], F32)
             grad_c = loaded.tile([P, PACK, UNITS], BF16)
             x_c = loaded.tile([P, PACK, FEATURES], BF16)
-            d2_hbm = d2[k_rows, :].rearrange("(p j) u -> p j u", j=PACK)
-            grad_hbm = grad_out[k_rows, :].rearrange("(p j) u -> p j u", j=PACK)
-            x_hbm = x[k_rows, :].rearrange("(p j) i -> p j i", j=PACK)
+            d2_hbm = d2[k_rows, :].rearrange("(j p) u -> p j u", j=PACK)
+            grad_hbm = grad_out[k_rows, :].rearrange("(j p) u -> p j u", j=PACK)
+            x_hbm = x[k_rows, :].rearrange("(v p e) i -> p v (e i)", v=2, e=2)
             if c == 0:
                 nc.sync.dma_start(out=d2_c[:, :, :STEP_COLS], in_=d2_hbm[:, :, :STEP_COLS])
-                nc.sync.dma_start(out=x_c[:], in_=x_hbm)
+                nc.sync.dma_start(out=x_c[:].rearrange("p (v e) i -> p v (e i)", e=2), in_=x_hbm)
                 nc.sync.dma_start(out=grad_c[:], in_=grad_hbm)
                 nc.sync.dma_start(out=d2_c[:, :, STEP_COLS:], in_=d2_hbm[:, :, STEP_COLS:])
             else:
                 nc.sync.dma_start(out=d2_c[:], in_=d2_hbm)
                 nc.sync.dma_start(out=grad_c[:], in_=grad_hbm)
-                nc.sync.dma_start(out=x_c[:], in_=x_hbm)
+                nc.sync.dma_start(out=x_c[:].rearrange("p (v e) i -> p v (e i)", e=2), in_=x_hbm)
             d2_rows.append(d2_c)
             grad_rows.append(grad_c)
             x_rows.append(x_c)
@@ -122,9 +122,7 @@ def tile_rbflayer_v_kernel(tc, x, centers, gamma_raw, d2, grad_out, out):
             return c, slice(h * STEP_COLS, (h + 1) * STEP_COLS)
 
         def t_cols(j):
-            h, e = divmod(j, 2)
-            block = 2 * e + h
-            return slice(block * P, (block + 1) * P)
+            return slice(j * P, (j + 1) * P)
 
         def mask_grad(s):
             c, h, cols = place(s)
@@ -198,10 +196,10 @@ def tile_rbflayer_v_kernel(tc, x, centers, gamma_raw, d2, grad_out, out):
             for n in range(PAIR):
                 m = h * PAIR + n
                 nc.vector.scalar_tensor_tensor(
-                    out=dz_t[s][:, n, :].rearrange("p (q e) -> p q e", e=2),
-                    in0=decays[s][:, n, :].rearrange("p (e q) -> p q e", e=2),
+                    out=dz_t[s][:, n, :],
+                    in0=decays[s][:, n, :],
                     scalar=two_gamma[:, m : m + 1],
-                    in1=grad_t[s][:, n, :].rearrange("p (e q) -> p q e", e=2),
+                    in1=grad_t[s][:, n, :],
                     op0=ALU.mult,
                     op1=ALU.mult,
                     accum_out=row_sums[:, m, c : c + 1],

@@ -228,9 +228,10 @@ def tile_rbflayer_v_kernel(tc, x, centers, gamma_raw, d2, grad_out, out):
             dz_grouped[s] = work.tile([P, STEP_COLS, PACK], BF16, name="dz_grouped", align_bytes=64)
             for units, back in zip(parts(s), dz_back[s]):
                 target = dz_grouped[s][:, units[0] * P : (units[-1] + 1) * P, :]
+                words = target.rearrange("p u j -> p (u j)").bitcast(F32)
                 nc.scalar.copy(
-                    out=target.rearrange("p u j -> p (u j)").bitcast(F32),
-                    in_=back.rearrange("p h u -> p u h"),
+                    out=words.rearrange("p (n i h) -> p n h i", i=2, h=2),
+                    in_=back.rearrange("p h (n i) -> p n h i", i=2),
                 )
 
         def quantise_dz(s):

@@ -60,8 +60,8 @@ def tile_rbflayer_v_kernel(tc, x, centers, gamma_raw, d2, grad_out, out):
             grad_hbm = grad_out[k_rows, :].rearrange("(j p) u -> p j u", j=PACK)
             x_hbm = x[k_rows, :].rearrange("(v p e) i -> p v (e i)", v=2, e=2)
             if c == 0:
-                nc.sync.dma_start(out=d2_c[:, :, :STEP_COLS], in_=d2_hbm[:, :, :STEP_COLS])
                 nc.sync.dma_start(out=x_c[:].rearrange("p (v e) i -> p v (e i)", e=2), in_=x_hbm)
+                nc.sync.dma_start(out=d2_c[:, :, :STEP_COLS], in_=d2_hbm[:, :, :STEP_COLS])
                 nc.sync.dma_start(out=grad_c[:], in_=grad_hbm)
                 nc.sync.dma_start(out=d2_c[:, :, STEP_COLS:], in_=d2_hbm[:, :, STEP_COLS:])
             else:
@@ -104,6 +104,7 @@ def tile_rbflayer_v_kernel(tc, x, centers, gamma_raw, d2, grad_out, out):
             {}, {}, {}, {}, {}, {}, {}, {},
         )
         neg_totals = {}
+        x_round = {}
 
         def place(s):
             c, h = ORDER[s]
@@ -115,7 +116,7 @@ def tile_rbflayer_v_kernel(tc, x, centers, gamma_raw, d2, grad_out, out):
         def x_turn(k):
             if k < STEPS_PER_ROUND:
                 return -STEPS
-            return k - 1 if k < X_HALVES - 4 else k - 2
+            return k - 2
 
         def x_place(k):
             c, h = divmod(k, STEPS_PER_ROUND)
@@ -138,10 +139,12 @@ def tile_rbflayer_v_kernel(tc, x, centers, gamma_raw, d2, grad_out, out):
 
         def regroup_x(s, vector_cols):
             c, cols = x_place(s)
-            x_grouped[s] = work.tile(
-                [P, STEP_COLS, PACK], BF16, name="x_grouped", align_bytes=64, bufs=3
-            )
-            target = x_grouped[s][:].rearrange("p (n i) j -> p n j i", i=4)
+            if s % 2 == 0:
+                x_round[s // 2] = work.tile(
+                    [P, FEATURES, PACK], BF16, name="x_round", align_bytes=64, bufs=3
+                )
+            x_grouped[s] = x_round[s // 2][:, cols, :]
+            target = x_grouped[s].rearrange("p (n i) j -> p n j i", i=4)
             source = x_rows[c][:, :, cols].rearrange("p j (n i) -> p n j i", i=4)
             split = vector_cols // 4
             nc.vector.tensor_copy(out=target[:, :split], in_=source[:, :split])
@@ -150,10 +153,12 @@ def tile_rbflayer_v_kernel(tc, x, centers, gamma_raw, d2, grad_out, out):
 
         def quantise_x(s):
             c, cols = x_place(s)
+            if s % 2 == 0:
+                return
             nc.vector.quantize_mx(
-                out=x_codes[:, c, cols].bitcast(E4M3_X4),
-                scales=x_scales[:, c, cols],
-                in_=x_grouped[s][:].rearrange("p i j -> p (i j)"),
+                out=x_codes[:, c, :].bitcast(E4M3_X4),
+                scales=x_scales[:, c, :],
+                in_=x_round[c][:].rearrange("p i j -> p (i j)"),
             )
 
         def transpose_d2(s):
@@ -294,6 +299,8 @@ def tile_rbflayer_v_kernel(tc, x, centers, gamma_raw, d2, grad_out, out):
 
         for k in range(STEPS_PER_ROUND):
             regroup_x(k, STEP_COLS)
+        for k in range(STEPS_PER_ROUND):
+            quantise_x(k)
         gamma = const.tile([P, UNIT_BLOCKS], F32)
         nc.vector.scalar_tensor_tensor(
             out=gamma[:], in0=raw[:], scalar=0.0, in1=log_term[:], op0=ALU.max, op1=ALU.add
@@ -302,10 +309,8 @@ def tile_rbflayer_v_kernel(tc, x, centers, gamma_raw, d2, grad_out, out):
         nc.vector.tensor_scalar_mul(out=neg_gamma[:], in0=gamma[:], scalar1=-1.0)
         two_gamma = const.tile([P, UNIT_BLOCKS], F32)
         nc.vector.tensor_scalar_mul(out=two_gamma[:], in0=gamma[:], scalar1=2.0)
+        mask_grad(0)
         for t in range(-2, STEPS + 1):
-            if t == -1:
-                for k in range(STEPS_PER_ROUND):
-                    quantise_x(k)
             run(multiply_dz, t)
             run(transpose_back, t)
             run(transpose_grad, t + 1)
@@ -313,7 +318,8 @@ def tile_rbflayer_v_kernel(tc, x, centers, gamma_raw, d2, grad_out, out):
             for k in range(X_HALVES):
                 if x_turn(k) == t - 1:
                     quantise_x(k)
-            run(mask_grad, t + 2)
+            if t + 2 >= 1:
+                run(mask_grad, t + 2)
             run(exponentials, t + 1)
             run(regroup_dz, t)
             for k in range(X_HALVES):

@@ -28,7 +28,7 @@ X_HALVES = STEPS
 ORDER = [(c, h) for c in range(ROUNDS - 2) for h in range(STEPS_PER_ROUND)] + [
     (c, h) for h in range(STEPS_PER_ROUND) for c in range(ROUNDS - 2, ROUNDS)
 ]
-X_VECTOR_COLS = 48
+X_VECTOR_COLS = 0
 
 FLOPS = 2 * ROWS * UNITS * FEATURES
 
@@ -104,7 +104,7 @@ def tile_rbflayer_v_kernel(tc, x, centers, gamma_raw, d2, grad_out, out):
             {}, {}, {}, {}, {}, {}, {}, {},
         )
         neg_totals = {}
-        x_round = {}
+        signs = {}
 
         def place(s):
             c, h = ORDER[s]
@@ -128,6 +128,11 @@ def tile_rbflayer_v_kernel(tc, x, centers, gamma_raw, d2, grad_out, out):
         def mask_grad(s):
             c, h, cols = place(s)
             masked_grad[s] = work.tile([P, PACK, STEP_COLS], BF16, name="masked_grad")
+            if s >= 2:
+                nc.vector.tensor_tensor(
+                    out=masked_grad[s][:], in0=signs[s][:], in1=grad_rows[c][:, :, cols], op=ALU.mult
+                )
+                return
             nc.vector.scalar_tensor_tensor(
                 out=masked_grad[s][:],
                 in0=d2_rows[c][:, :, cols],
@@ -137,28 +142,38 @@ def tile_rbflayer_v_kernel(tc, x, centers, gamma_raw, d2, grad_out, out):
                 op1=ALU.mult,
             )
 
+        def take_sign(s):
+            c, h, cols = place(s)
+            if s >= 2:
+                signs[s] = work.tile([P, PACK, STEP_COLS], BF16, name="signs")
+                nc.scalar.activation(out=signs[s][:], in_=d2_rows[c][:, :, cols], func=ACT.Sign)
+
         def regroup_x(s, vector_cols):
             c, cols = x_place(s)
-            if s % 2 == 0:
-                x_round[s // 2] = work.tile(
-                    [P, FEATURES, PACK], BF16, name="x_round", align_bytes=64, bufs=3
+            x_grouped[s] = work.tile(
+                [P, STEP_COLS, PACK], BF16, name="x_grouped", align_bytes=64, bufs=2
+            )
+            if vector_cols:
+                nc.vector.tensor_copy(
+                    out=x_grouped[s][:].rearrange("p (n i) j -> p n j i", i=4),
+                    in_=x_rows[c][:, :, cols].rearrange("p j (n i) -> p n j i", i=4),
                 )
-            x_grouped[s] = x_round[s // 2][:, cols, :]
-            target = x_grouped[s].rearrange("p (n i) j -> p n j i", i=4)
-            source = x_rows[c][:, :, cols].rearrange("p j (n i) -> p n j i", i=4)
-            split = vector_cols // 4
-            nc.vector.tensor_copy(out=target[:, :split], in_=source[:, :split])
-            if vector_cols < STEP_COLS:
-                nc.scalar.copy(out=target[:, split:], in_=source[:, split:])
+            else:
+                nc.gpsimd.tensor_scalar(
+                    out=x_grouped[s][:],
+                    in0=x_rows[c][:, :, cols].rearrange("p j i -> p i j"),
+                    scalar1=1.0,
+                    scalar2=0.0,
+                    op0=ALU.mult,
+                    op1=ALU.add,
+                )
 
         def quantise_x(s):
             c, cols = x_place(s)
-            if s % 2 == 0:
-                return
             nc.vector.quantize_mx(
-                out=x_codes[:, c, :].bitcast(E4M3_X4),
-                scales=x_scales[:, c, :],
-                in_=x_round[c][:].rearrange("p i j -> p (i j)"),
+                out=x_codes[:, c, cols].bitcast(E4M3_X4),
+                scales=x_scales[:, c, cols],
+                in_=x_grouped[s][:].rearrange("p i j -> p (i j)"),
             )
 
         def transpose_d2(s):
@@ -234,10 +249,12 @@ def tile_rbflayer_v_kernel(tc, x, centers, gamma_raw, d2, grad_out, out):
             for units, back in zip(parts(s), dz_back[s]):
                 target = dz_grouped[s][:, units[0] * P : (units[-1] + 1) * P, :]
                 words = target.rearrange("p u j -> p (u j)").bitcast(F32)
-                nc.scalar.copy(
-                    out=words.rearrange("p (n i h) -> p n h i", i=2, h=2),
-                    in_=back.rearrange("p h (n i) -> p n h i", i=2),
-                )
+                to = words.rearrange("p (n i h) -> p n h i", i=2, h=2)
+                source = back.rearrange("p h (n i) -> p n h i", i=2)
+                if s % 3 == 1 and s < STEPS - 1:
+                    nc.vector.tensor_copy(out=to, in_=source)
+                else:
+                    nc.scalar.copy(out=to, in_=source)
 
         def quantise_dz(s):
             c, h, cols = place(s)
@@ -310,18 +327,19 @@ def tile_rbflayer_v_kernel(tc, x, centers, gamma_raw, d2, grad_out, out):
         two_gamma = const.tile([P, UNIT_BLOCKS], F32)
         nc.vector.tensor_scalar_mul(out=two_gamma[:], in0=gamma[:], scalar1=2.0)
         mask_grad(0)
-        for t in range(-2, STEPS + 1):
+        for t in range(-3, STEPS + 1):
             run(multiply_dz, t)
             run(transpose_back, t)
             run(transpose_grad, t + 1)
             run(quantise_dz, t - 1)
+            if t + 2 >= 1:
+                run(mask_grad, t + 2)
             for k in range(X_HALVES):
                 if x_turn(k) == t - 1:
                     quantise_x(k)
-            if t + 2 >= 1:
-                run(mask_grad, t + 2)
             run(exponentials, t + 1)
             run(regroup_dz, t)
+            run(take_sign, t + 3)
             for k in range(X_HALVES):
                 if x_turn(k) == t:
                     regroup_x(k, X_VECTOR_COLS)

@@ -25,9 +25,7 @@ STEP_COLS = PAIR * P
 STEPS_PER_ROUND = UNIT_BLOCKS // PAIR
 STEPS = ROUNDS * STEPS_PER_ROUND
 X_HALVES = STEPS
-ORDER = [(c, h) for c in range(ROUNDS - 2) for h in range(STEPS_PER_ROUND)] + [
-    (c, h) for h in range(STEPS_PER_ROUND) for c in range(ROUNDS - 2, ROUNDS)
-]
+ORDER = [(c, h) for c in range(ROUNDS) for h in range(STEPS_PER_ROUND)]
 X_VECTOR_COLS = 0
 
 FLOPS = 2 * ROWS * UNITS * FEATURES
@@ -64,6 +62,11 @@ def tile_rbflayer_v_kernel(tc, x, centers, gamma_raw, d2, grad_out, out):
                 nc.sync.dma_start(out=d2_c[:, :, :STEP_COLS], in_=d2_hbm[:, :, :STEP_COLS])
                 nc.sync.dma_start(out=grad_c[:], in_=grad_hbm)
                 nc.sync.dma_start(out=d2_c[:, :, STEP_COLS:], in_=d2_hbm[:, :, STEP_COLS:])
+            elif c == 1:
+                nc.sync.dma_start(out=d2_c[:, :, :STEP_COLS], in_=d2_hbm[:, :, :STEP_COLS])
+                nc.sync.dma_start(out=grad_c[:], in_=grad_hbm)
+                nc.sync.dma_start(out=d2_c[:, :, STEP_COLS:], in_=d2_hbm[:, :, STEP_COLS:])
+                nc.sync.dma_start(out=x_c[:].rearrange("p (v e) i -> p v (e i)", e=2), in_=x_hbm)
             else:
                 nc.sync.dma_start(out=d2_c[:], in_=d2_hbm)
                 nc.sync.dma_start(out=grad_c[:], in_=grad_hbm)
@@ -116,7 +119,7 @@ def tile_rbflayer_v_kernel(tc, x, centers, gamma_raw, d2, grad_out, out):
         def x_turn(k):
             if k < STEPS_PER_ROUND:
                 return -STEPS
-            return k - 2
+            return k - 1
 
         def x_place(k):
             c, h = divmod(k, STEPS_PER_ROUND)
@@ -128,7 +131,7 @@ def tile_rbflayer_v_kernel(tc, x, centers, gamma_raw, d2, grad_out, out):
         def mask_grad(s):
             c, h, cols = place(s)
             masked_grad[s] = work.tile([P, PACK, STEP_COLS], BF16, name="masked_grad")
-            if s >= 2:
+            if s >= 3:
                 nc.vector.tensor_tensor(
                     out=masked_grad[s][:], in0=signs[s][:], in1=grad_rows[c][:, :, cols], op=ALU.mult
                 )
@@ -144,7 +147,7 @@ def tile_rbflayer_v_kernel(tc, x, centers, gamma_raw, d2, grad_out, out):
 
         def take_sign(s):
             c, h, cols = place(s)
-            if s >= 2:
+            if s >= 3:
                 signs[s] = work.tile([P, PACK, STEP_COLS], BF16, name="signs")
                 nc.scalar.activation(out=signs[s][:], in_=d2_rows[c][:, :, cols], func=ACT.Sign)
 
@@ -153,7 +156,7 @@ def tile_rbflayer_v_kernel(tc, x, centers, gamma_raw, d2, grad_out, out):
             x_grouped[s] = work.tile(
                 [P, STEP_COLS, PACK], BF16, name="x_grouped", align_bytes=64, bufs=2
             )
-            if vector_cols:
+            if vector_cols or s in (2,):
                 nc.vector.tensor_copy(
                     out=x_grouped[s][:].rearrange("p (n i) j -> p n j i", i=4),
                     in_=x_rows[c][:, :, cols].rearrange("p j (n i) -> p n j i", i=4),
@@ -251,7 +254,7 @@ def tile_rbflayer_v_kernel(tc, x, centers, gamma_raw, d2, grad_out, out):
                 words = target.rearrange("p u j -> p (u j)").bitcast(F32)
                 to = words.rearrange("p (n i h) -> p n h i", i=2, h=2)
                 source = back.rearrange("p h (n i) -> p n h i", i=2)
-                if s % 3 == 1 and s < STEPS - 1:
+                if (s % 2 == 1) and s < STEPS - 1:
                     nc.vector.tensor_copy(out=to, in_=source)
                 else:
                     nc.scalar.copy(out=to, in_=source)
@@ -332,11 +335,11 @@ def tile_rbflayer_v_kernel(tc, x, centers, gamma_raw, d2, grad_out, out):
             run(transpose_back, t)
             run(transpose_grad, t + 1)
             run(quantise_dz, t - 1)
-            if t + 2 >= 1:
-                run(mask_grad, t + 2)
             for k in range(X_HALVES):
                 if x_turn(k) == t - 1:
                     quantise_x(k)
+            if t + 2 >= 1:
+                run(mask_grad, t + 2)
             run(exponentials, t + 1)
             run(regroup_dz, t)
             run(take_sign, t + 3)

@@ -54,11 +54,11 @@ def tile_rbflayer_v_kernel(tc, x, centers, gamma_raw, d2, grad_out, out):
             d2_c = loaded.tile([P, PACK, UNITS], F32)
             grad_c = loaded.tile([P, PACK, UNITS], BF16)
             x_c = loaded.tile([P, PACK, FEATURES], BF16)
-            d2_hbm = d2[k_rows, :].rearrange("(j p) u -> p j u", j=PACK)
-            grad_hbm = grad_out[k_rows, :].rearrange("(j p) u -> p j u", j=PACK)
-            x_hbm = x[k_rows, :].rearrange("(v p e) i -> p v (e i)", v=2, e=2)
+            d2_hbm = d2[k_rows, :].rearrange("(p j) u -> p j u", j=PACK)
+            grad_hbm = grad_out[k_rows, :].rearrange("(p j) u -> p j u", j=PACK)
+            x_hbm = x[k_rows, :].rearrange("(p j) i -> p j i", j=PACK)
             if c == 0:
-                nc.sync.dma_start(out=x_c[:].rearrange("p (v e) i -> p v (e i)", e=2), in_=x_hbm)
+                nc.sync.dma_start(out=x_c[:], in_=x_hbm)
                 nc.sync.dma_start(out=d2_c[:, :, :STEP_COLS], in_=d2_hbm[:, :, :STEP_COLS])
                 nc.sync.dma_start(out=grad_c[:], in_=grad_hbm)
                 nc.sync.dma_start(out=d2_c[:, :, STEP_COLS:], in_=d2_hbm[:, :, STEP_COLS:])
@@ -66,11 +66,11 @@ def tile_rbflayer_v_kernel(tc, x, centers, gamma_raw, d2, grad_out, out):
                 nc.sync.dma_start(out=d2_c[:, :, :STEP_COLS], in_=d2_hbm[:, :, :STEP_COLS])
                 nc.sync.dma_start(out=grad_c[:], in_=grad_hbm)
                 nc.sync.dma_start(out=d2_c[:, :, STEP_COLS:], in_=d2_hbm[:, :, STEP_COLS:])
-                nc.sync.dma_start(out=x_c[:].rearrange("p (v e) i -> p v (e i)", e=2), in_=x_hbm)
+                nc.sync.dma_start(out=x_c[:], in_=x_hbm)
             else:
                 nc.sync.dma_start(out=d2_c[:], in_=d2_hbm)
                 nc.sync.dma_start(out=grad_c[:], in_=grad_hbm)
-                nc.sync.dma_start(out=x_c[:].rearrange("p (v e) i -> p v (e i)", e=2), in_=x_hbm)
+                nc.sync.dma_start(out=x_c[:], in_=x_hbm)
             d2_rows.append(d2_c)
             grad_rows.append(grad_c)
             x_rows.append(x_c)
@@ -126,7 +126,9 @@ def tile_rbflayer_v_kernel(tc, x, centers, gamma_raw, d2, grad_out, out):
             return c, slice(h * STEP_COLS, (h + 1) * STEP_COLS)
 
         def t_cols(j):
-            return slice(j * P, (j + 1) * P)
+            h, e = divmod(j, 2)
+            block = 2 * e + h
+            return slice(block * P, (block + 1) * P)
 
         def mask_grad(s):
             c, h, cols = place(s)
@@ -219,10 +221,10 @@ def tile_rbflayer_v_kernel(tc, x, centers, gamma_raw, d2, grad_out, out):
             for n in range(PAIR):
                 m = h * PAIR + n
                 nc.vector.scalar_tensor_tensor(
-                    out=dz_t[s][:, n, :],
-                    in0=decays[s][:, n, :],
+                    out=dz_t[s][:, n, :].rearrange("p (q e) -> p q e", e=2),
+                    in0=decays[s][:, n, :].rearrange("p (e q) -> p q e", e=2),
                     scalar=two_gamma[:, m : m + 1],
-                    in1=grad_t[s][:, n, :],
+                    in1=grad_t[s][:, n, :].rearrange("p (e q) -> p q e", e=2),
                     op0=ALU.mult,
                     op1=ALU.mult,
                     accum_out=row_sums[:, m, c : c + 1],
@@ -341,8 +343,8 @@ def tile_rbflayer_v_kernel(tc, x, centers, gamma_raw, d2, grad_out, out):
             if t + 2 >= 1:
                 run(mask_grad, t + 2)
             run(exponentials, t + 1)
-            run(regroup_dz, t)
             run(take_sign, t + 3)
+            run(regroup_dz, t)
             for k in range(X_HALVES):
                 if x_turn(k) == t:
                     regroup_x(k, X_VECTOR_COLS)

from contextlib import ExitStack

import concourse.mybir as mybir
from concourse.masks import make_identity

F32 = mybir.dt.float32
BF16 = mybir.dt.bfloat16
U32 = mybir.dt.uint32
U8 = mybir.dt.uint8
E4M3_X4 = mybir.dt.float8_e4m3fn_x4
E5M2_X4 = mybir.dt.float8_e5m2_x4
ALU = mybir.AluOpType
ACT = mybir.ActivationFunctionType

ROWS = 3072
UNITS = 512
FEATURES = 512
P = 128
PACK = 4
K_PASS = P * PACK
ROUNDS = ROWS // K_PASS
UNIT_BLOCKS = UNITS // P
PAIR = 2
STEP_COLS = PAIR * P
STEPS_PER_ROUND = UNIT_BLOCKS // PAIR
STEPS = ROUNDS * STEPS_PER_ROUND
X_HALVES = STEPS
ORDER = [(c, h) for c in range(ROUNDS) for h in range(STEPS_PER_ROUND)]
X_VECTOR_COLS = 0

FLOPS = 2 * ROWS * UNITS * FEATURES


def tile_rbflayer_v_kernel(tc, x, centers, gamma_raw, d2, grad_out, out):
    nc = tc.nc
    with ExitStack() as stack:
        const = stack.enter_context(tc.tile_pool(name="const", bufs=1))
        loaded = stack.enter_context(tc.tile_pool(name="loaded", bufs=ROUNDS))
        work = stack.enter_context(tc.tile_pool(name="work", bufs=2))
        psum_out = stack.enter_context(tc.psum_pool(name="psum_out", bufs=1))
        psum_d2 = stack.enter_context(tc.psum_pool(name="psum_d2", bufs=PAIR))
        psum_grad = stack.enter_context(tc.psum_pool(name="psum_grad", bufs=1))
        psum_back = stack.enter_context(tc.psum_pool(name="psum_back", bufs=1))
        stack.enter_context(tc.manual_schedule())

        gamma_rows = const.tile([P, P], BF16)
        nc.vector.memset(gamma_rows[:], 0.0)
        nc.sync.dma_start(
            out=gamma_rows[0:UNIT_BLOCKS, :], in_=gamma_raw.rearrange("(m p) -> m p", p=P)
        )
        d2_rows, grad_rows, x_rows = [], [], []
        for c in range(ROUNDS):
            k_rows = slice(c * K_PASS, (c + 1) * K_PASS)
            d2_c = loaded.tile([P, PACK, UNITS], F32)
            grad_c = loaded.tile([P, PACK, UNITS], BF16)
            x_c = loaded.tile([P, PACK, FEATURES], BF16)
            d2_hbm = d2[k_rows, :].rearrange("(p j) u -> p j u", j=PACK)
            grad_hbm = grad_out[k_rows, :].rearrange("(p j) u -> p j u", j=PACK)
            x_hbm = x[k_rows, :].rearrange("(p j) i -> p j i", j=PACK)
            if c == 0:
                nc.sync.dma_start(out=x_c[:], in_=x_hbm)
                nc.sync.dma_start(out=d2_c[:, :, :STEP_COLS], in_=d2_hbm[:, :, :STEP_COLS])
                nc.sync.dma_start(out=grad_c[:], in_=grad_hbm)
                nc.sync.dma_start(out=d2_c[:, :, STEP_COLS:], in_=d2_hbm[:, :, STEP_COLS:])
            elif c == 1:
                nc.sync.dma_start(out=d2_c[:, :, :STEP_COLS], in_=d2_hbm[:, :, :STEP_COLS])
                nc.sync.dma_start(out=grad_c[:], in_=grad_hbm)
                nc.sync.dma_start(out=d2_c[:, :, STEP_COLS:], in_=d2_hbm[:, :, STEP_COLS:])
                nc.sync.dma_start(out=x_c[:], in_=x_hbm)
            else:
                nc.sync.dma_start(out=d2_c[:], in_=d2_hbm)
                nc.sync.dma_start(out=grad_c[:], in_=grad_hbm)
                nc.sync.dma_start(out=x_c[:], in_=x_hbm)
            d2_rows.append(d2_c)
            grad_rows.append(grad_c)
            x_rows.append(x_c)
        centers_sb = const.tile([P, UNIT_BLOCKS, FEATURES], BF16)
        nc.sync.dma_start(out=centers_sb[:], in_=centers.rearrange("(m p) i -> p m i", p=P))

        ident_bf16 = const.tile([P, P], BF16)
        make_identity(nc, ident_bf16[:])
        ident_f32 = const.tile([P, P], F32)
        make_identity(nc, ident_f32[:])

        gamma_cols = psum_back.tile([P, P], BF16, tag="back")
        nc.tensor.transpose(gamma_cols[:], gamma_rows[:], ident_bf16[:])
        raw = const.tile([P, UNIT_BLOCKS], F32)
        nc.vector.tensor_copy(out=raw[:], in_=gamma_cols[:, 0:UNIT_BLOCKS])
        magnitude = const.tile([P, UNIT_BLOCKS], F32)
        nc.scalar.activation(out=magnitude[:], in_=raw[:], func=ACT.Abs)
        decay = const.tile([P, UNIT_BLOCKS], F32)
        nc.scalar.activation(out=decay[:], in_=magnitude[:], func=ACT.Exp, scale=-1.0)
        log_term = const.tile([P, UNIT_BLOCKS], F32)
        nc.scalar.activation(out=log_term[:], in_=decay[:], func=ACT.Ln, bias=1.0)
        warm = const.tile([P, UNIT_BLOCKS], F32)
        nc.scalar.activation(out=warm[:], in_=decay[:], func=ACT.Exp)
        dz_codes = const.tile([P, ROUNDS, UNITS], U32, align_bytes=64)
        dz_scales = const.tile([P, ROUNDS, UNITS], U8, align_bytes=64)
        x_codes = const.tile([P, ROUNDS, FEATURES], U32, align_bytes=64)
        x_scales = const.tile([P, ROUNDS, FEATURES], U8, align_bytes=64)
        row_sums = const.tile([P, UNIT_BLOCKS, ROUNDS], F32)
        products = []
        for m in range(UNIT_BLOCKS):
            products.append(psum_out.tile([P, FEATURES], F32, name="products%d" % m))

        masked_grad, x_grouped, d2_t, grad_t, decays, dz_t, dz_back, dz_grouped = (
            {}, {}, {}, {}, {}, {}, {}, {},
        )
        neg_totals = {}
        signs = {}

        def place(s):
            c, h = ORDER[s]
            return c, h, slice(h * STEP_COLS, (h + 1) * STEP_COLS)

        def parts(s):
            return [[n] for n in range(PAIR)] if s == STEPS - 1 else [list(range(PAIR))]

        def x_turn(k):
            if k < STEPS_PER_ROUND:
                return -STEPS
            return k - 1

        def x_place(k):
            c, h = divmod(k, STEPS_PER_ROUND)
            return c, slice(h * STEP_COLS, (h + 1) * STEP_COLS)

        def t_cols(j):
            h, e = divmod(j, 2)
            block = 2 * e + h
            return slice(block * P, (block + 1) * P)

        def mask_grad(s):
            c, h, cols = place(s)
            masked_grad[s] = work.tile([P, PACK, STEP_COLS], BF16, name="masked_grad")
            if s >= 3:
                nc.vector.tensor_tensor(
                    out=masked_grad[s][:], in0=signs[s][:], in1=grad_rows[c][:, :, cols], op=ALU.mult
                )
                return
            nc.vector.scalar_tensor_tensor(
                out=masked_grad[s][:],
                in0=d2_rows[c][:, :, cols],
                scalar=0.0,
                in1=grad_rows[c][:, :, cols],
                op0=ALU.is_gt,
                op1=ALU.mult,
            )

        def take_sign(s):
            c, h, cols = place(s)
            if s >= 3:
                signs[s] = work.tile([P, PACK, STEP_COLS], BF16, name="signs")
                nc.scalar.activation(out=signs[s][:], in_=d2_rows[c][:, :, cols], func=ACT.Sign)

        def regroup_x(s, vector_cols):
            c, cols = x_place(s)
            x_grouped[s] = work.tile(
                [P, STEP_COLS, PACK], BF16, name="x_grouped", align_bytes=64, bufs=2
            )
            if vector_cols or s in (2,):
                nc.vector.tensor_copy(
                    out=x_grouped[s][:].rearrange("p (n i) j -> p n j i", i=4),
                    in_=x_rows[c][:, :, cols].rearrange("p j (n i) -> p n j i", i=4),
                )
            else:
                nc.gpsimd.tensor_scalar(
                    out=x_grouped[s][:],
                    in0=x_rows[c][:, :, cols].rearrange("p j i -> p i j"),
                    scalar1=1.0,
                    scalar2=0.0,
                    op0=ALU.mult,
                    op1=ALU.add,
                )

        def quantise_x(s):
            c, cols = x_place(s)
            nc.vector.quantize_mx(
                out=x_codes[:, c, cols].bitcast(E4M3_X4),
                scales=x_scales[:, c, cols],
                in_=x_grouped[s][:].rearrange("p i j -> p (i j)"),
            )

        def transpose_d2(s):
            c, h, cols = place(s)
            for n in range(PAIR):
                m = h * PAIR + n
                d2_t[s, n] = psum_d2.tile([P, K_PASS], F32, name="d2_t")
                for j in range(PACK):
                    nc.tensor.transpose(
                        d2_t[s, n][:, t_cols(j)],
                        d2_rows[c][:, j, m * P : (m + 1) * P],
                        ident_f32[:],
                    )

        def transpose_grad(s):
            grad_t[s] = psum_grad.tile([P, PAIR, K_PASS], BF16, name="grad_t")
            for n in range(PAIR):
                for j in range(PACK):
                    nc.tensor.transpose(
                        grad_t[s][:, n, t_cols(j)],
                        masked_grad[s][:, j, n * P : (n + 1) * P],
                        ident_bf16[:],
                    )

        def exponentials(s):
            c, h, cols = place(s)
            decays[s] = work.tile([P, PAIR, K_PASS], F32, name="decays")
            for n in range(PAIR):
                m = h * PAIR + n
                nc.scalar.activation(
                    out=decays[s][:, n, :],
                    in_=d2_t[s, n][:],
                    func=ACT.Exp,
                    scale=neg_gamma[:, m : m + 1],
                )

        def multiply_dz(s):
            c, h, cols = place(s)
            dz_t[s] = work.tile([P, PAIR, K_PASS], BF16, name="dz_t")
            for n in range(PAIR):
                m = h * PAIR + n
                nc.vector.scalar_tensor_tensor(
                    out=dz_t[s][:, n, :].rearrange("p (q e) -> p q e", e=2),
                    in0=decays[s][:, n, :].rearrange("p (e q) -> p q e", e=2),
                    scalar=two_gamma[:, m : m + 1],
                    in1=grad_t[s][:, n, :].rearrange("p (e q) -> p q e", e=2),
                    op0=ALU.mult,
                    op1=ALU.mult,
                    accum_out=row_sums[:, m, c : c + 1],
                )

        def transpose_back(s):
            dz_back[s] = []
            for units in parts(s):
                if s < STEPS - 1:
                    bank = psum_back.tile([P, K_PASS], F32, name="dz_back", tag="back")
                else:
                    bank = psum_d2.tile([P, K_PASS], F32, name="d2_t")
                width = len(units) * P
                back = bank[:, : 2 * width].rearrange("p (h u) -> p h u", u=width)
                for i, n in enumerate(units):
                    words = dz_t[s][:, n, :].bitcast(F32)
                    for h in range(PACK // 2):
                        nc.tensor.transpose(
                            back[:, h, i * P : (i + 1) * P],
                            words[:, h * P : (h + 1) * P],
                            ident_f32[:],
                        )
                dz_back[s].append(back)

        def regroup_dz(s):
            dz_grouped[s] = work.tile([P, STEP_COLS, PACK], BF16, name="dz_grouped", align_bytes=64)
            for units, back in zip(parts(s), dz_back[s]):
                target = dz_grouped[s][:, units[0] * P : (units[-1] + 1) * P, :]
                words = target.rearrange("p u j -> p (u j)").bitcast(F32)
                to = words.rearrange("p (n i h) -> p n h i", i=2, h=2)
                source = back.rearrange("p h (n i) -> p n h i", i=2)
                if (s % 2 == 1) and s < STEPS - 1:
                    nc.vector.tensor_copy(out=to, in_=source)
                else:
                    nc.scalar.copy(out=to, in_=source)

        def quantise_dz(s):
            c, h, cols = place(s)
            for units in parts(s):
                source = dz_grouped[s][:, units[0] * P : (units[-1] + 1) * P, :]
                unit_cols = slice(cols.start + units[0] * P, cols.start + (units[-1] + 1) * P)
                nc.vector.quantize_mx(
                    out=dz_codes[:, c, unit_cols].bitcast(E5M2_X4),
                    scales=dz_scales[:, c, unit_cols],
                    in_=source.rearrange("p u j -> p (u j)"),
                )

        def matmul_round(s):
            c, h, cols = place(s)
            for n in range(PAIR):
                m = h * PAIR + n
                unit_cols = slice(m * P, (m + 1) * P)
                nc.tensor.matmul_mx(
                    out=products[m][:],
                    lhsT=dz_codes[:, c, unit_cols].bitcast(E5M2_X4),
                    lhsT_scale=dz_scales[:, c, unit_cols],
                    rhs=x_codes[:, c, :].bitcast(E4M3_X4),
                    rhs_scale=x_scales[:, c, :],
                    start=(c == 0),
                    stop=(c == ROUNDS - 1),
                )

        def center_term(s):
            c, h, cols = place(s)
            blocks = slice(h * PAIR, (h + 1) * PAIR)
            totals = work.tile([P, PAIR], F32, name="totals")
            nc.vector.tensor_reduce(
                out=totals[:], in_=row_sums[:, blocks, :], axis=mybir.AxisListType.X, op=ALU.add
            )
            neg_totals[h] = work.tile([P, PAIR], F32, name="neg_totals")
            nc.vector.tensor_scalar_mul(out=neg_totals[h][:], in0=totals[:], scalar1=-1.0)

        def store_out(blocks):
            for m in blocks:
                h, n = divmod(m, PAIR)
                result = work.tile([P, FEATURES], F32, name="result", bufs=UNIT_BLOCKS)
                nc.vector.scalar_tensor_tensor(
                    out=result[:],
                    in0=centers_sb[:, m, :],
                    scalar=neg_totals[h][:, n : n + 1],
                    in1=products[m][:],
                    op0=ALU.mult,
                    op1=ALU.add,
                )
                nc.sync.dma_start(out=out[m * P : (m + 1) * P, :], in_=result[:])

        def run(stage, s):
            if 0 <= s < STEPS:
                stage(s)

        def run_last_round(stage, s):
            if 0 <= s < STEPS and ORDER[s][0] == ROUNDS - 1:
                stage(s)

        for k in range(STEPS_PER_ROUND):
            regroup_x(k, STEP_COLS)
        for k in range(STEPS_PER_ROUND):
            quantise_x(k)
        gamma = const.tile([P, UNIT_BLOCKS], F32)
        nc.vector.scalar_tensor_tensor(
            out=gamma[:], in0=raw[:], scalar=0.0, in1=log_term[:], op0=ALU.max, op1=ALU.add
        )
        neg_gamma = const.tile([P, UNIT_BLOCKS], F32)
        nc.vector.tensor_scalar_mul(out=neg_gamma[:], in0=gamma[:], scalar1=-1.0)
        two_gamma = const.tile([P, UNIT_BLOCKS], F32)
        nc.vector.tensor_scalar_mul(out=two_gamma[:], in0=gamma[:], scalar1=2.0)
        mask_grad(0)
        for t in range(-3, STEPS + 1):
            run(multiply_dz, t)
            run(transpose_back, t)
            run(transpose_grad, t + 1)
            run(quantise_dz, t - 1)
            for k in range(X_HALVES):
                if x_turn(k) == t - 1:
                    quantise_x(k)
            if t + 2 >= 1:
                run(mask_grad, t + 2)
            run(exponentials, t + 1)
            run(take_sign, t + 3)
            run(regroup_dz, t)
            for k in range(X_HALVES):
                if x_turn(k) == t:
                    regroup_x(k, X_VECTOR_COLS)
            run_last_round(center_term, t)
            run(transpose_d2, t + 2)
            run(matmul_round, t - 1)
            if t == STEPS - 1:
                store_out([0])
            elif t == STEPS:
                store_out(range(1, UNIT_BLOCKS))
